import numpy as np
import ml_dtypes


def mxq(x, axis, fmt="e4m3"):
    dtype, down = {"e4m3": (ml_dtypes.float8_e4m3fn, 7), "e5m2": (ml_dtypes.float8_e5m2, 14)}[fmt]
    v = np.moveaxis(np.asarray(x, np.float32).astype(ml_dtypes.bfloat16).astype(np.float64), axis, -1)
    blocks = v.reshape(v.shape[:-1] + (-1, 32))
    amax = np.abs(blocks).max(-1, keepdims=True)
    byte = np.maximum(np.where(amax > 0, np.frexp(amax)[1] - 1 + 127, 0) - down, 1)
    scale = np.exp2(byte - 127.0)
    codes = (blocks / scale).astype(np.float32).astype(dtype).astype(np.float64)
    return np.moveaxis((codes * scale).reshape(v.shape), -1, axis)


WIDE = False


def mx_kscale(k):
    if not WIDE:
        return np.ones(k)
    levels = np.array([10, -10, 5, -5, 0])
    if k % 512:
        return np.exp2(np.random.permutation(np.resize(levels, k // 32))).repeat(32)
    a = np.empty((k // 512, 16))
    for p in range(k // 512):
        a[p, :8] = np.random.permutation(np.resize(levels, 8))
        for g in range(8):
            far = levels[np.abs(levels - a[p, g]) >= 10]
            a[p, g + 8] = far[np.random.randint(len(far))]
    return np.exp2(a.ravel()).repeat(32)


BF16 = ml_dtypes.bfloat16


def bf(x):
    return np.asarray(x, np.float32).astype(BF16)


def f64(x):
    return np.asarray(x).astype(np.float64)


T, D, F, R = 512, 1024, 2560, 128


def draw0():
    s = mx_kscale(F)
    return {
        "h": bf(np.random.standard_normal((T, F)) * 0.75 * s),
        "ha": bf(np.random.standard_normal((T, R)) * 0.75),
        "W_down": bf(np.random.standard_normal((F, D)) / np.sqrt(F) / s[:, None]),
        "B_down": bf(np.random.standard_normal((R, D)) * 0.5 / np.sqrt(R)),
    }


def core(h, ha, W_down, B_down):
    return (mxq(f64(h), 1, "e4m3") @ mxq(f64(W_down), 0, "e4m3")) + f64(ha) @ f64(B_down)


def e4m3fn_bytes(y):
    return np.clip(np.asarray(y, np.float64), -448.0, 448.0).astype(np.float32).astype(ml_dtypes.float8_e4m3fn).view(np.uint8)


def e4m3fn_values(b):
    return np.asarray(b, np.uint8).view(ml_dtypes.float8_e4m3fn).astype(np.float64)


def setup_inputs():
    d = draw0()
    x0 = np.asarray(d['W_down']).astype(np.float64)
    s = (np.max(np.abs(x0), axis=(1,), keepdims=True) / 448.0).astype(np.float32)
    out = {}
    for k, v in d.items():
        if k == 'W_down':
            out['W_down_bytes'] = e4m3fn_bytes(x0 / s.astype(np.float64))
            out['W_down_scale'] = s
        else:
            out[k] = v
    return out


def reference(h, ha, W_down_bytes, W_down_scale, B_down):
    return core(h, ha, e4m3fn_values(W_down_bytes) * W_down_scale.astype(np.float64), B_down)

@@ -1,0 +1,233 @@
+from contextlib import ExitStack
+
+import concourse.mybir as mybir
+from concourse.masks import make_identity
+
+T, D, F, R = 512, 1024, 2560, 128
+FLOPS = 2 * T * F * D + 2 * T * R * D
+
+F32 = mybir.dt.float32
+BF16 = mybir.dt.bfloat16
+U32 = mybir.dt.uint32
+U8 = mybir.dt.uint8
+FP8 = mybir.dt.float8_e4m3fn
+FP8X4 = mybir.dt.float8_e4m3fn_x4
+COPY = mybir.ActivationFunctionType.Copy
+MULT = mybir.AluOpType.mult
+ADD = mybir.AluOpType.add
+
+P = 128
+PACK = 4
+K_PASS = P * PACK
+PASSES = F // K_PASS
+M_TILES = T // P
+N_TILE = 512
+HALVES = D // N_TILE
+UNITS = PASSES * HALVES
+
+V_PLANES = [2, 2, 1, 1, 1, 1, 1, 1, 1, 1]
+QH_LAG = 1
+LORA0_COPY_AT = {2: (0, 1), 3: (2, 3)}
+FINAL0_AT = {6: (0,), 7: (1, 2), 8: (3,)}
+LORA1_COPY_AT = {9: (0, 1, 2, 3)}
+
+
+def tile_loramlp_pb_kernel(tc, h, ha, W_down_bytes, W_down_scale, B_down, out):
+    nc = tc.nc
+    with ExitStack() as ctx:
+        keep = ctx.enter_context(tc.tile_pool(name="keep", bufs=1))
+        stage = ctx.enter_context(tc.tile_pool(name="stage", bufs=4))
+        psum = ctx.enter_context(tc.psum_pool(name="psum", bufs=1))
+        ctx.enter_context(tc.manual_schedule())
+
+        def bank(b, shape, dtype, name):
+            return psum.tile(shape, dtype, tag="bank%d" % b, name=name)
+
+        w_view = W_down_bytes.rearrange("(g p t) n -> g p t n", p=P, t=PACK)
+        h_view = h.rearrange("(m p) k -> p m k", p=P)
+        w_scale = keep.tile([P, PASSES, PACK], F32, name="w_scale")
+        w_bytes = {}
+        h_rows = {}
+
+        def load_w(u):
+            g, hf = u % PASSES, u // PASSES
+            w_bytes[u] = keep.tile([P, PACK, N_TILE], U8, name="w_bytes%d" % u)
+            nc.sync.dma_start(out=w_bytes[u][:], in_=w_view[g][:, :, hf * N_TILE : (hf + 1) * N_TILE])
+
+        def load_h(g):
+            h_rows[g] = keep.tile([P, M_TILES, K_PASS], BF16, name="h_rows%d" % g)
+            nc.sync.dma_start(out=h_rows[g][:], in_=h_view[:, :, g * K_PASS : (g + 1) * K_PASS])
+
+        nc.sync.dma_start(out=w_scale[:], in_=W_down_scale.rearrange("(g p t) o -> p g (t o)", p=P, t=PACK))
+        load_w(0)
+        load_w(1)
+        load_h(0)
+        load_w(2)
+        ha_rows = keep.tile([P, M_TILES, R], BF16, name="ha_rows")
+        nc.sync.dma_start(out=ha_rows[:], in_=ha.rearrange("(m p) r -> p m r", p=P))
+        b_sb = keep.tile([P, D], BF16, name="b_sb")
+        nc.sync.dma_start(out=b_sb[:], in_=B_down)
+        load_h(1)
+        load_w(3)
+        load_h(2)
+        load_w(4)
+        load_h(3)
+        load_w(5)
+        load_h(4)
+        for u in range(6, UNITS):
+            load_w(u)
+
+        ident_f32 = keep.tile([P, P], F32, name="ident_f32")
+        make_identity(nc, ident_f32[:])
+        ident_bf16 = keep.tile([P, P], BF16, name="ident_bf16")
+        make_identity(nc, ident_bf16[:])
+        warm_in = keep.tile([P, 1], F32, name="warm_in")
+        warm_out = keep.tile([P, 1], F32, name="warm_out")
+        nc.vector.memset(warm_in[:], 0.0)
+        nc.scalar.activation(out=warm_out[:], in_=warm_in[:], func=COPY)
+
+        wide = {}
+        grouped = {}
+        w_codes = {}
+        w_scl = {}
+
+        def widen(u):
+            g = u % PASSES
+            wide[u] = stage.tile([P, PACK, N_TILE], BF16, tag="wide", name="wide%d" % u)
+            for t in range(PACK):
+                src = w_bytes[u][:, t, :].bitcast(FP8)
+                if t < PACK - V_PLANES[u]:
+                    nc.scalar.activation(out=wide[u][:, t, :], in_=src, func=COPY, scale=w_scale[:, g, t : t + 1])
+                else:
+                    nc.vector.tensor_scalar(out=wide[u][:, t, :], in0=src, scalar1=w_scale[:, g, t : t + 1], scalar2=None, op0=MULT)
+
+        def interleave(u):
+            grouped[u] = stage.tile([P, N_TILE, PACK], BF16, tag="grouped", name="grouped%d" % u, align_bytes=64)
+            nc.vector.tensor_copy(out=grouped[u][:], in_=wide[u][:].rearrange("p t c -> p c t"))
+
+        def quantize_w(u):
+            w_codes[u] = keep.tile([P, N_TILE], U32, name="w_codes%d" % u, align_bytes=64)
+            w_scl[u] = keep.tile([P, N_TILE], U8, name="w_scl%d" % u, align_bytes=64)
+            nc.vector.quantize_mx(
+                out=w_codes[u][:].bitcast(FP8X4),
+                scales=w_scl[u][:],
+                in_=grouped[u][:].rearrange("p c t -> p (c t)"),
+            )
+
+        scratch = [4]
+        h_ps = {}
+        h_grouped = {}
+        h_codes = {}
+        h_scl = {}
+
+        def next_scratch():
+            b = scratch[0]
+            scratch[0] = 4 + (b - 3) % 4
+            return b
+
+        def transpose_h(g):
+            for j in range(2):
+                h_ps[(g, j)] = bank(next_scratch(), [P, 2, 2 * P], F32, "h_ps%d_%d" % (g, j))
+                for mm in range(2):
+                    words = h_rows[g][:, 2 * j + mm, :].bitcast(F32)
+                    for e in range(2):
+                        nc.tensor.transpose(h_ps[(g, j)][:, e, mm * P : (mm + 1) * P], words[:, e : K_PASS // 2 : 2], ident_f32[:])
+
+        def copy_h(g):
+            h_grouped[g] = stage.tile([P, T * PACK], BF16, tag="h_grouped", name="h_grouped%d" % g, align_bytes=64)
+            for j in range(2):
+                dst = h_grouped[g][:, j * 1024 : (j + 1) * 1024].bitcast(F32).rearrange("p (q e) -> p q e", e=2)
+                nc.scalar.copy(out=dst, in_=h_ps[(g, j)][:].rearrange("p e q -> p q e"))
+
+        def quantize_h(g):
+            h_codes[g] = keep.tile([P, T], U32, name="h_codes%d" % g, align_bytes=64)
+            h_scl[g] = keep.tile([P, T], U8, name="h_scl%d" % g, align_bytes=64)
+            nc.vector.quantize_mx(out=h_codes[g][:].bitcast(FP8X4), scales=h_scl[g][:], in_=h_grouped[g][:])
+
+        haT = keep.tile([P, T], BF16, name="haT")
+        haT_ps = {}
+        lora_ps = {}
+        lora = {}
+
+        def transpose_ha():
+            haT_ps[0] = bank(next_scratch(), [P, M_TILES, P], BF16, "haT_ps")
+            for m in range(M_TILES):
+                nc.tensor.transpose(haT_ps[0][:, m, :], ha_rows[:, m, :], ident_bf16[:])
+
+        def copy_haT():
+            nc.scalar.copy(out=haT[:], in_=haT_ps[0][:].rearrange("p m t -> p (m t)"))
+
+        def lora_matmul(m, hf):
+            lora_ps[(m, hf)] = bank(m, [P, N_TILE], F32, "lora_ps%d_%d" % (m, hf))
+            nc.tensor.matmul(
+                lora_ps[(m, hf)][:],
+                lhsT=haT[:, m * P : (m + 1) * P],
+                rhs=b_sb[:, hf * N_TILE : (hf + 1) * N_TILE],
+                start=True,
+                stop=True,
+            )
+
+        def lora_copy(m, hf):
+            lora[(m, hf)] = keep.tile([P, N_TILE], F32, name="lora%d_%d" % (m, hf))
+            nc.scalar.copy(out=lora[(m, hf)][:], in_=lora_ps[(m, hf)][:])
+
+        acc = {}
+
+        def mx(u):
+            g, hf = u % PASSES, u // PASSES
+            for m in range(M_TILES):
+                if g == 0:
+                    acc[(m, hf)] = bank(4 * hf + m, [P, N_TILE], F32, "acc%d_%d" % (m, hf))
+                nc.tensor.matmul_mx(
+                    out=acc[(m, hf)][:],
+                    lhsT=h_codes[g][:, m * P : (m + 1) * P].bitcast(FP8X4),
+                    lhsT_scale=h_scl[g][:, m * P : (m + 1) * P],
+                    rhs=w_codes[u][:].bitcast(FP8X4),
+                    rhs_scale=w_scl[u][:],
+                    start=(g == 0),
+                    stop=(g == PASSES - 1),
+                )
+
+        def final(m, hf):
+            res = stage.tile([P, N_TILE], F32, tag="res", name="res%d_%d" % (m, hf))
+            nc.vector.tensor_tensor(out=res[:], in0=acc[(m, hf)][:], in1=lora[(m, hf)][:], op=ADD)
+            nc.sync.dma_start(out=out[m * P : (m + 1) * P, hf * N_TILE : (hf + 1) * N_TILE], in_=res[:])
+
+        widen(0)
+        widen(1)
+        transpose_h(0)
+        transpose_ha()
+        interleave(0)
+        for u in range(UNITS):
+            if u + 2 < UNITS:
+                widen(u + 2)
+            if u < PASSES:
+                copy_h(u)
+                if u == 0:
+                    copy_haT()
+                if u + 1 < PASSES:
+                    transpose_h(u + 1)
+                if u == 1:
+                    for m in range(M_TILES):
+                        lora_matmul(m, 0)
+            for m in LORA0_COPY_AT.get(u, ()):
+                lora_copy(m, 0)
+            if u + 1 < UNITS and u != UNITS - 2:
+                interleave(u + 1)
+            if 0 <= u - QH_LAG < PASSES:
+                quantize_h(u - QH_LAG)
+            quantize_w(u)
+            if u == UNITS - 2:
+                interleave(u + 1)
+            if u == PASSES - 1 + QH_LAG:
+                for v in range(u + 1):
+                    mx(v)
+            if u > PASSES - 1 + QH_LAG:
+                mx(u)
+            for m in FINAL0_AT.get(u, ()):
+                final(m, 0)
+                lora_matmul(m, 1)
+            for m in LORA1_COPY_AT.get(u, ()):
+                lora_copy(m, 1)
+        for m in range(M_TILES):
+            final(m, 1)

@@ -103,7 +103,10 @@ def tile_loramlp_pb_kernel(tc, h, ha, W_down_bytes, W_down_scale, B_down, out):
 
         def interleave(u):
             grouped[u] = stage.tile([P, N_TILE, PACK], BF16, tag="grouped", name="grouped%d" % u, align_bytes=64)
-            nc.vector.tensor_copy(out=grouped[u][:], in_=wide[u][:].rearrange("p t c -> p c t"))
+            nc.vector.tensor_copy(
+                out=grouped[u][:].rearrange("p (c i) t -> p c t i", i=4),
+                in_=wide[u][:].rearrange("p t (c i) -> p c t i", i=4),
+            )
 
         def quantize_w(u):
             w_codes[u] = keep.tile([P, N_TILE], U32, name="w_codes%d" % u, align_bytes=64)

@@ -25,11 +25,15 @@ N_TILE = 512
 HALVES = D // N_TILE
 UNITS = PASSES * HALVES
 
-V_PLANES = [2, 2, 1, 1, 1, 1, 1, 1, 1, 1]
-QH_LAG = 1
-LORA0_COPY_AT = {2: (0, 1), 3: (2, 3)}
-FINAL0_AT = {6: (0,), 7: (1, 2), 8: (3,)}
-LORA1_COPY_AT = {9: (0, 1, 2, 3)}
+V_PLANES = [2, 2, 2, 1, 1, 2, 2, 2, 1, 0]
+S_INTERLEAVES = (7,)
+S_LEAD = 2
+H_LAG = 1
+QH_LAG = 2
+HA_AT = 2
+LORA0_COPY_AT = 4
+FINAL0_AT = 7
+MX_AT = [4, 4, 5, 6, 7, 7, 7, 7, 8, 9]
 
 
 def tile_loramlp_pb_kernel(tc, h, ha, W_down_bytes, W_down_scale, B_down, out):
@@ -44,38 +48,54 @@ def tile_loramlp_pb_kernel(tc, h, ha, W_down_bytes, W_down_scale, B_down, out):
             return psum.tile(shape, dtype, tag="bank%d" % b, name=name)
 
         w_view = W_down_bytes.rearrange("(g p t) n -> g p t n", p=P, t=PACK)
+        s_view = W_down_scale.rearrange("(g p t) o -> g p (t o)", p=P, t=PACK)
         h_view = h.rearrange("(m p) k -> p m k", p=P)
-        w_scale = keep.tile([P, PASSES, PACK], F32, name="w_scale")
-        w_bytes = {}
+        w_scale = {}
+        w_plane = {}
         h_rows = {}
 
-        def load_w(u):
+        def load_scale(g):
+            w_scale[g] = keep.tile([P, PACK], F32, name="w_scale%d" % g)
+            nc.sync.dma_start(out=w_scale[g][:], in_=s_view[g])
+
+        def load_w(u, pieces):
             g, hf = u % PASSES, u // PASSES
-            w_bytes[u] = keep.tile([P, PACK, N_TILE], U8, name="w_bytes%d" % u)
-            nc.sync.dma_start(out=w_bytes[u][:], in_=w_view[g][:, :, hf * N_TILE : (hf + 1) * N_TILE])
+            cols = slice(hf * N_TILE, (hf + 1) * N_TILE)
+            for i in range(pieces):
+                w_bytes = keep.tile([P, PACK // pieces, N_TILE], U8, name="w_bytes%d_%d" % (u, i))
+                nc.sync.dma_start(out=w_bytes[:], in_=w_view[g][:, i : PACK : pieces, cols])
+                for j in range(PACK // pieces):
+                    w_plane[(u, i + j * pieces)] = w_bytes[:, j, :]
 
         def load_h(g):
             h_rows[g] = keep.tile([P, M_TILES, K_PASS], BF16, name="h_rows%d" % g)
             nc.sync.dma_start(out=h_rows[g][:], in_=h_view[:, :, g * K_PASS : (g + 1) * K_PASS])
 
-        nc.sync.dma_start(out=w_scale[:], in_=W_down_scale.rearrange("(g p t) o -> p g (t o)", p=P, t=PACK))
-        load_w(0)
-        load_w(1)
-        load_h(0)
-        load_w(2)
         ha_rows = keep.tile([P, M_TILES, R], BF16, name="ha_rows")
-        nc.sync.dma_start(out=ha_rows[:], in_=ha.rearrange("(m p) r -> p m r", p=P))
         b_sb = keep.tile([P, D], BF16, name="b_sb")
-        nc.sync.dma_start(out=b_sb[:], in_=B_down)
+
+        load_scale(0)
+        load_w(0, 2)
+        load_scale(1)
+        load_w(1, 1)
+        load_scale(2)
+        load_w(2, 1)
+        load_h(0)
+        load_scale(3)
+        load_w(3, 1)
         load_h(1)
-        load_w(3)
+        load_scale(4)
+        load_w(4, 1)
+        nc.sync.dma_start(out=ha_rows[:], in_=ha.rearrange("(m p) r -> p m r", p=P))
+        nc.sync.dma_start(out=b_sb[:], in_=B_down)
         load_h(2)
-        load_w(4)
+        load_w(5, 1)
         load_h(3)
-        load_w(5)
+        load_w(6, 1)
         load_h(4)
-        for u in range(6, UNITS):
-            load_w(u)
+        load_w(7, 1)
+        load_w(8, 1)
+        load_w(9, 1)
 
         ident_f32 = keep.tile([P, P], F32, name="ident_f32")
         make_identity(nc, ident_f32[:])
@@ -91,22 +111,25 @@ def tile_loramlp_pb_kernel(tc, h, ha, W_down_bytes, W_down_scale, B_down, out):
         w_codes = {}
         w_scl = {}
 
-        def widen(u):
+        def widen_s(u):
             g = u % PASSES
             wide[u] = stage.tile([P, PACK, N_TILE], BF16, tag="wide", name="wide%d" % u)
-            for t in range(PACK):
-                src = w_bytes[u][:, t, :].bitcast(FP8)
-                if t < PACK - V_PLANES[u]:
-                    nc.scalar.activation(out=wide[u][:, t, :], in_=src, func=COPY, scale=w_scale[:, g, t : t + 1])
-                else:
-                    nc.vector.tensor_scalar(out=wide[u][:, t, :], in0=src, scalar1=w_scale[:, g, t : t + 1], scalar2=None, op0=MULT)
+            for t in range(PACK - V_PLANES[u]):
+                nc.scalar.activation(out=wide[u][:, t, :], in_=w_plane[(u, t)].bitcast(FP8), func=COPY, scale=w_scale[g][:, t : t + 1])
+
+        def widen_v(u):
+            g = u % PASSES
+            for t in range(PACK - V_PLANES[u], PACK):
+                nc.vector.tensor_scalar(out=wide[u][:, t, :], in0=w_plane[(u, t)].bitcast(FP8), scalar1=w_scale[g][:, t : t + 1], scalar2=None, op0=MULT)
 
         def interleave(u):
             grouped[u] = stage.tile([P, N_TILE, PACK], BF16, tag="grouped", name="grouped%d" % u, align_bytes=64)
-            nc.vector.tensor_copy(
-                out=grouped[u][:].rearrange("p (c i) t -> p c t i", i=4),
-                in_=wide[u][:].rearrange("p t (c i) -> p c t i", i=4),
-            )
+            dst = grouped[u][:].rearrange("p (c i) t -> p c t i", i=4)
+            src = wide[u][:].rearrange("p t (c i) -> p c t i", i=4)
+            if u in S_INTERLEAVES:
+                nc.scalar.copy(out=dst, in_=src)
+            else:
+                nc.vector.tensor_copy(out=dst, in_=src)
 
         def quantize_w(u):
             w_codes[u] = keep.tile([P, N_TILE], U32, name="w_codes%d" % u, align_bytes=64)
@@ -160,8 +183,8 @@ def tile_loramlp_pb_kernel(tc, h, ha, W_down_bytes, W_down_scale, B_down, out):
         def copy_haT():
             nc.scalar.copy(out=haT[:], in_=haT_ps[0][:].rearrange("p m t -> p (m t)"))
 
-        def lora_matmul(m, hf):
-            lora_ps[(m, hf)] = bank(m, [P, N_TILE], F32, "lora_ps%d_%d" % (m, hf))
+        def lora_matmul(m, hf, b):
+            lora_ps[(m, hf)] = bank(b, [P, N_TILE], F32, "lora_ps%d_%d" % (m, hf))
             nc.tensor.matmul(
                 lora_ps[(m, hf)][:],
                 lhsT=haT[:, m * P : (m + 1) * P],
@@ -196,41 +219,56 @@ def tile_loramlp_pb_kernel(tc, h, ha, W_down_bytes, W_down_scale, B_down, out):
             nc.vector.tensor_tensor(out=res[:], in0=acc[(m, hf)][:], in1=lora[(m, hf)][:], op=ADD)
             nc.sync.dma_start(out=out[m * P : (m + 1) * P, hf * N_TILE : (hf + 1) * N_TILE], in_=res[:])
 
-        widen(0)
-        widen(1)
+        for v in range(S_LEAD):
+            widen_s(v)
+        widen_v(0)
+        widen_v(1)
         transpose_h(0)
-        transpose_ha()
         interleave(0)
         for u in range(UNITS):
+            if u + S_LEAD < UNITS:
+                widen_s(u + S_LEAD)
             if u + 2 < UNITS:
-                widen(u + 2)
-            if u < PASSES:
-                copy_h(u)
-                if u == 0:
-                    copy_haT()
-                if u + 1 < PASSES:
-                    transpose_h(u + 1)
-                if u == 1:
-                    for m in range(M_TILES):
-                        lora_matmul(m, 0)
-            for m in LORA0_COPY_AT.get(u, ()):
-                lora_copy(m, 0)
-            if u + 1 < UNITS and u != UNITS - 2:
+                widen_v(u + 2)
+            if 0 <= u - H_LAG < PASSES:
+                copy_h(u - H_LAG)
+                if u - H_LAG + 1 < PASSES:
+                    transpose_h(u - H_LAG + 1)
+            if u == HA_AT:
+                transpose_ha()
+            if u == HA_AT + 1:
+                copy_haT()
+                for m in range(M_TILES):
+                    lora_matmul(m, 0, m)
+            if u == LORA0_COPY_AT:
+                for m in range(M_TILES):
+                    lora_copy(m, 0)
+            if u == FINAL0_AT + 1:
+                lora_copy(0, 1)
+                lora_copy(1, 1)
+            if u == FINAL0_AT + 2:
+                lora_copy(2, 1)
+                lora_copy(3, 1)
+            if u < UNITS - 2:
                 interleave(u + 1)
             if 0 <= u - QH_LAG < PASSES:
                 quantize_h(u - QH_LAG)
             quantize_w(u)
             if u == UNITS - 2:
                 interleave(u + 1)
-            if u == PASSES - 1 + QH_LAG:
-                for v in range(u + 1):
+                final(2, 0)
+            for v in range(UNITS):
+                if MX_AT[v] == u:
                     mx(v)
-            if u > PASSES - 1 + QH_LAG:
-                mx(u)
-            for m in FINAL0_AT.get(u, ()):
-                final(m, 0)
-                lora_matmul(m, 1)
-            for m in LORA1_COPY_AT.get(u, ()):
-                lora_copy(m, 1)
+            if u == FINAL0_AT + 1:
+                lora_matmul(2, 1, 0)
+                lora_matmul(3, 1, 1)
+            if u == UNITS - 1:
+                final(3, 0)
+            if u == FINAL0_AT:
+                final(0, 0)
+                final(1, 0)
+                lora_matmul(0, 1, 0)
+                lora_matmul(1, 1, 1)
         for m in range(M_TILES):
             final(m, 1)

@@ -42,7 +42,6 @@ def tile_loramlp_pb_kernel(tc, h, ha, W_down_bytes, W_down_scale, B_down, out):
         keep = ctx.enter_context(tc.tile_pool(name="keep", bufs=1))
         stage = ctx.enter_context(tc.tile_pool(name="stage", bufs=4))
         psum = ctx.enter_context(tc.psum_pool(name="psum", bufs=1))
-        ctx.enter_context(tc.manual_schedule())
 
         def bank(b, shape, dtype, name):
             return psum.tile(shape, dtype, tag="bank%d" % b, name=name)

@@ -25,15 +25,16 @@ N_TILE = 512
 HALVES = D // N_TILE
 UNITS = PASSES * HALVES
 
-V_PLANES = [2, 2, 2, 1, 1, 2, 2, 2, 1, 0]
-S_INTERLEAVES = (7,)
+V_PLANES = [2, 2, 1, 1, 1, 1, 1, 1, 1, 0]
+S_INTERLEAVES = ()
 S_LEAD = 2
 H_LAG = 1
 QH_LAG = 2
-HA_AT = 2
-LORA0_COPY_AT = 4
+HA_AT = 4
+LORA0_AT = 5
+LORA0_COPY_AT = 6
 FINAL0_AT = 7
-MX_AT = [4, 4, 5, 6, 7, 7, 7, 7, 8, 9]
+MX_AT = [2, 3, 4, 5, 6, 6, 6, 7, 8, 9]
 
 
 def tile_loramlp_pb_kernel(tc, h, ha, W_down_bytes, W_down_scale, B_down, out):
@@ -42,6 +43,7 @@ def tile_loramlp_pb_kernel(tc, h, ha, W_down_bytes, W_down_scale, B_down, out):
         keep = ctx.enter_context(tc.tile_pool(name="keep", bufs=1))
         stage = ctx.enter_context(tc.tile_pool(name="stage", bufs=4))
         psum = ctx.enter_context(tc.psum_pool(name="psum", bufs=1))
+        ctx.enter_context(tc.manual_schedule())
 
         def bank(b, shape, dtype, name):
             return psum.tile(shape, dtype, tag="bank%d" % b, name=name)
@@ -85,14 +87,14 @@ def tile_loramlp_pb_kernel(tc, h, ha, W_down_bytes, W_down_scale, B_down, out):
         load_h(1)
         load_scale(4)
         load_w(4, 1)
-        nc.sync.dma_start(out=ha_rows[:], in_=ha.rearrange("(m p) r -> p m r", p=P))
-        nc.sync.dma_start(out=b_sb[:], in_=B_down)
         load_h(2)
         load_w(5, 1)
         load_h(3)
         load_w(6, 1)
         load_h(4)
         load_w(7, 1)
+        nc.sync.dma_start(out=ha_rows[:], in_=ha.rearrange("(m p) r -> p m r", p=P))
+        nc.sync.dma_start(out=b_sb[:], in_=B_down)
         load_w(8, 1)
         load_w(9, 1)
 
@@ -237,8 +239,6 @@ def tile_loramlp_pb_kernel(tc, h, ha, W_down_bytes, W_down_scale, B_down, out):
                 transpose_ha()
             if u == HA_AT + 1:
                 copy_haT()
-                for m in range(M_TILES):
-                    lora_matmul(m, 0, m)
             if u == LORA0_COPY_AT:
                 for m in range(M_TILES):
                     lora_copy(m, 0)
@@ -259,6 +259,9 @@ def tile_loramlp_pb_kernel(tc, h, ha, W_down_bytes, W_down_scale, B_down, out):
             for v in range(UNITS):
                 if MX_AT[v] == u:
                     mx(v)
+            if u == LORA0_AT:
+                for m in range(M_TILES):
+                    lora_matmul(m, 0, 4 + m)
             if u == FINAL0_AT + 1:
                 lora_matmul(2, 1, 0)
                 lora_matmul(3, 1, 1)

@@ -216,7 +216,7 @@ def tile_loramlp_pb_kernel(tc, h, ha, W_down_bytes, W_down_scale, B_down, out):
                 )
 
         def final(m, hf):
-            res = stage.tile([P, N_TILE], F32, tag="res", name="res%d_%d" % (m, hf))
+            res = keep.tile([P, N_TILE], F32, name="res%d_%d" % (m, hf))
             nc.vector.tensor_tensor(out=res[:], in0=acc[(m, hf)][:], in1=lora[(m, hf)][:], op=ADD)
             nc.sync.dma_start(out=out[m * P : (m + 1) * P, hf * N_TILE : (hf + 1) * N_TILE], in_=res[:])
 

@@ -26,7 +26,7 @@ HALVES = D // N_TILE
 UNITS = PASSES * HALVES
 
 V_PLANES = [2, 2, 1, 1, 1, 1, 1, 1, 1, 0]
-S_INTERLEAVES = ()
+V_COLS_LAST = 320
 S_LEAD = 2
 H_LAG = 1
 QH_LAG = 2
@@ -123,14 +123,18 @@ def tile_loramlp_pb_kernel(tc, h, ha, W_down_bytes, W_down_scale, B_down, out):
             for t in range(PACK - V_PLANES[u], PACK):
                 nc.vector.tensor_scalar(out=wide[u][:, t, :], in0=w_plane[(u, t)].bitcast(FP8), scalar1=w_scale[g][:, t : t + 1], scalar2=None, op0=MULT)
 
-        def interleave(u):
+        def interleave_part(u, copy, lo, hi):
+            copy(
+                out=grouped[u][:, lo:hi, :].rearrange("p (c i) t -> p c t i", i=4),
+                in_=wide[u][:, :, lo:hi].rearrange("p t (c i) -> p c t i", i=4),
+            )
+
+        def new_grouped(u):
             grouped[u] = stage.tile([P, N_TILE, PACK], BF16, tag="grouped", name="grouped%d" % u, align_bytes=64)
-            dst = grouped[u][:].rearrange("p (c i) t -> p c t i", i=4)
-            src = wide[u][:].rearrange("p t (c i) -> p c t i", i=4)
-            if u in S_INTERLEAVES:
-                nc.scalar.copy(out=dst, in_=src)
-            else:
-                nc.vector.tensor_copy(out=dst, in_=src)
+
+        def interleave(u):
+            new_grouped(u)
+            interleave_part(u, nc.vector.tensor_copy, 0, N_TILE)
 
         def quantize_w(u):
             w_codes[u] = keep.tile([P, N_TILE], U32, name="w_codes%d" % u, align_bytes=64)
@@ -200,9 +204,9 @@ def tile_loramlp_pb_kernel(tc, h, ha, W_down_bytes, W_down_scale, B_down, out):
 
         acc = {}
 
-        def mx(u):
+        def mx(u, tiles=(0, 1, 2, 3)):
             g, hf = u % PASSES, u // PASSES
-            for m in range(M_TILES):
+            for m in tiles:
                 if g == 0:
                     acc[(m, hf)] = bank(4 * hf + m, [P, N_TILE], F32, "acc%d_%d" % (m, hf))
                 nc.tensor.matmul_mx(
@@ -242,31 +246,35 @@ def tile_loramlp_pb_kernel(tc, h, ha, W_down_bytes, W_down_scale, B_down, out):
             if u == LORA0_COPY_AT:
                 for m in range(M_TILES):
                     lora_copy(m, 0)
+            if u == UNITS - 2:
+                new_grouped(u + 1)
+                interleave_part(u + 1, nc.scalar.copy, V_COLS_LAST, N_TILE)
             if u == FINAL0_AT + 1:
                 lora_copy(0, 1)
                 lora_copy(1, 1)
-            if u == FINAL0_AT + 2:
-                lora_copy(2, 1)
-                lora_copy(3, 1)
             if u < UNITS - 2:
                 interleave(u + 1)
             if 0 <= u - QH_LAG < PASSES:
                 quantize_h(u - QH_LAG)
             quantize_w(u)
             if u == UNITS - 2:
-                interleave(u + 1)
+                interleave_part(u + 1, nc.vector.tensor_copy, 0, V_COLS_LAST)
                 final(2, 0)
-            for v in range(UNITS):
+            for v in range(UNITS - 1):
                 if MX_AT[v] == u:
                     mx(v)
             if u == LORA0_AT:
                 for m in range(M_TILES):
                     lora_matmul(m, 0, 4 + m)
-            if u == FINAL0_AT + 1:
-                lora_matmul(2, 1, 0)
-                lora_matmul(3, 1, 1)
+            if u == UNITS - 2:
+                lora_matmul(2, 1, 2)
             if u == UNITS - 1:
+                lora_copy(2, 1)
                 final(3, 0)
+                mx(u, (0, 1))
+                lora_matmul(3, 1, 3)
+                mx(u, (2, 3))
+                lora_copy(3, 1)
             if u == FINAL0_AT:
                 final(0, 0)
                 final(1, 0)

@@ -25,7 +25,7 @@ N_TILE = 512
 HALVES = D // N_TILE
 UNITS = PASSES * HALVES
 
-V_PLANES = [2, 2, 1, 1, 1, 1, 1, 1, 1, 0]
+V_PLANES = [2, 2, 1, 1, 1, 1, 1, 1, 2, 0]
 V_COLS_LAST = 320
 S_LEAD = 2
 H_LAG = 1

@@ -26,7 +26,7 @@ HALVES = D // N_TILE
 UNITS = PASSES * HALVES
 
 V_PLANES = [2, 2, 1, 1, 1, 1, 1, 1, 2, 0]
-V_COLS_LAST = 320
+V_COLS_LAST = 256
 S_LEAD = 2
 H_LAG = 1
 QH_LAG = 2
@@ -231,14 +231,17 @@ def tile_loramlp_pb_kernel(tc, h, ha, W_down_bytes, W_down_scale, B_down, out):
         transpose_h(0)
         interleave(0)
         for u in range(UNITS):
+            if u - H_LAG == PASSES - 1:
+                copy_h(PASSES - 1)
+            if u - QH_LAG == PASSES - 1:
+                quantize_h(PASSES - 1)
             if u + S_LEAD < UNITS:
                 widen_s(u + S_LEAD)
             if u + 2 < UNITS:
                 widen_v(u + 2)
-            if 0 <= u - H_LAG < PASSES:
+            if 0 <= u - H_LAG < PASSES - 1:
                 copy_h(u - H_LAG)
-                if u - H_LAG + 1 < PASSES:
-                    transpose_h(u - H_LAG + 1)
+                transpose_h(u - H_LAG + 1)
             if u == HA_AT:
                 transpose_ha()
             if u == HA_AT + 1:
@@ -254,7 +257,7 @@ def tile_loramlp_pb_kernel(tc, h, ha, W_down_bytes, W_down_scale, B_down, out):
                 lora_copy(1, 1)
             if u < UNITS - 2:
                 interleave(u + 1)
-            if 0 <= u - QH_LAG < PASSES:
+            if 0 <= u - QH_LAG < PASSES - 1:
                 quantize_h(u - QH_LAG)
             quantize_w(u)
             if u == UNITS - 2:

@@ -63,17 +63,17 @@ def tile_loramlp_pb_kernel(tc, h, ha, W_down_bytes, W_down_scale, B_down, out):
             g, hf = u % PASSES, u // PASSES
             cols = slice(hf * N_TILE, (hf + 1) * N_TILE)
             for i in range(pieces):
-                w_bytes = keep.tile([P, PACK // pieces, N_TILE], U8, name="w_bytes%d_%d" % (u, i))
+                w_bytes = keep.tile([P, PACK // pieces, N_TILE], U8, name="w_bytes%d_%d" % (u, i), align_bytes=256)
                 nc.sync.dma_start(out=w_bytes[:], in_=w_view[g][:, i : PACK : pieces, cols])
                 for j in range(PACK // pieces):
                     w_plane[(u, i + j * pieces)] = w_bytes[:, j, :]
 
         def load_h(g):
-            h_rows[g] = keep.tile([P, M_TILES, K_PASS], BF16, name="h_rows%d" % g)
+            h_rows[g] = keep.tile([P, M_TILES, K_PASS], BF16, name="h_rows%d" % g, align_bytes=256)
             nc.sync.dma_start(out=h_rows[g][:], in_=h_view[:, :, g * K_PASS : (g + 1) * K_PASS])
 
-        ha_rows = keep.tile([P, M_TILES, R], BF16, name="ha_rows")
-        b_sb = keep.tile([P, D], BF16, name="b_sb")
+        ha_rows = keep.tile([P, M_TILES, R], BF16, name="ha_rows", align_bytes=256)
+        b_sb = keep.tile([P, D], BF16, name="b_sb", align_bytes=256)
 
         load_scale(0)
         load_w(0, 2)
@@ -220,7 +220,7 @@ def tile_loramlp_pb_kernel(tc, h, ha, W_down_bytes, W_down_scale, B_down, out):
                 )
 
         def final(m, hf):
-            res = keep.tile([P, N_TILE], F32, name="res%d_%d" % (m, hf))
+            res = keep.tile([P, N_TILE], F32, name="res%d_%d" % (m, hf), align_bytes=256)
             nc.vector.tensor_tensor(out=res[:], in0=acc[(m, hf)][:], in1=lora[(m, hf)][:], op=ADD)
             nc.sync.dma_start(out=out[m * P : (m + 1) * P, hf * N_TILE : (hf + 1) * N_TILE], in_=res[:])
 

@@ -78,7 +78,7 @@ def tile_loramlp_pb_kernel(tc, h, ha, W_down_bytes, W_down_scale, B_down, out):
         load_scale(0)
         load_w(0, 2)
         load_scale(1)
-        load_w(1, 1)
+        load_w(1, 2)
         load_scale(2)
         load_w(2, 1)
         load_h(0)

@@ -26,7 +26,7 @@ HALVES = D // N_TILE
 UNITS = PASSES * HALVES
 
 V_PLANES = [2, 2, 1, 1, 1, 1, 1, 1, 2, 0]
-V_COLS_LAST = 256
+V_COLS_LAST = 224
 S_LEAD = 2
 H_LAG = 1
 QH_LAG = 2
@@ -67,6 +67,8 @@ def tile_loramlp_pb_kernel(tc, h, ha, W_down_bytes, W_down_scale, B_down, out):
                 nc.sync.dma_start(out=w_bytes[:], in_=w_view[g][:, i : PACK : pieces, cols])
                 for j in range(PACK // pieces):
                     w_plane[(u, i + j * pieces)] = w_bytes[:, j, :]
+                if hf == 0 and i == 0:
+                    load_scale(g)
 
         def load_h(g):
             h_rows[g] = keep.tile([P, M_TILES, K_PASS], BF16, name="h_rows%d" % g, align_bytes=256)
@@ -75,17 +77,12 @@ def tile_loramlp_pb_kernel(tc, h, ha, W_down_bytes, W_down_scale, B_down, out):
         ha_rows = keep.tile([P, M_TILES, R], BF16, name="ha_rows", align_bytes=256)
         b_sb = keep.tile([P, D], BF16, name="b_sb", align_bytes=256)
 
-        load_scale(0)
         load_w(0, 2)
-        load_scale(1)
         load_w(1, 2)
-        load_scale(2)
         load_w(2, 1)
         load_h(0)
-        load_scale(3)
         load_w(3, 1)
         load_h(1)
-        load_scale(4)
         load_w(4, 1)
         load_h(2)
         load_w(5, 1)

@@ -26,7 +26,7 @@ HALVES = D // N_TILE
 UNITS = PASSES * HALVES
 
 V_PLANES = [2, 2, 1, 1, 1, 1, 1, 1, 2, 0]
-V_COLS_LAST = 224
+V_COLS_LAST = 256
 S_LEAD = 2
 H_LAG = 1
 QH_LAG = 2
@@ -111,7 +111,7 @@ def tile_loramlp_pb_kernel(tc, h, ha, W_down_bytes, W_down_scale, B_down, out):
 
         def widen_s(u):
             g = u % PASSES
-            wide[u] = stage.tile([P, PACK, N_TILE], BF16, tag="wide", name="wide%d" % u)
+            wide[u] = stage.tile([P, PACK, N_TILE], BF16, tag="wide", name="wide%d" % u, align_bytes=256)
             for t in range(PACK - V_PLANES[u]):
                 nc.scalar.activation(out=wide[u][:, t, :], in_=w_plane[(u, t)].bitcast(FP8), func=COPY, scale=w_scale[g][:, t : t + 1])
 
@@ -127,15 +127,15 @@ def tile_loramlp_pb_kernel(tc, h, ha, W_down_bytes, W_down_scale, B_down, out):
             )
 
         def new_grouped(u):
-            grouped[u] = stage.tile([P, N_TILE, PACK], BF16, tag="grouped", name="grouped%d" % u, align_bytes=64)
+            grouped[u] = stage.tile([P, N_TILE, PACK], BF16, tag="grouped", name="grouped%d" % u, align_bytes=256)
 
         def interleave(u):
             new_grouped(u)
             interleave_part(u, nc.vector.tensor_copy, 0, N_TILE)
 
         def quantize_w(u):
-            w_codes[u] = keep.tile([P, N_TILE], U32, name="w_codes%d" % u, align_bytes=64)
-            w_scl[u] = keep.tile([P, N_TILE], U8, name="w_scl%d" % u, align_bytes=64)
+            w_codes[u] = keep.tile([P, N_TILE], U32, name="w_codes%d" % u, align_bytes=256)
+            w_scl[u] = keep.tile([P, N_TILE], U8, name="w_scl%d" % u, align_bytes=256)
             nc.vector.quantize_mx(
                 out=w_codes[u][:].bitcast(FP8X4),
                 scales=w_scl[u][:],
@@ -162,17 +162,17 @@ def tile_loramlp_pb_kernel(tc, h, ha, W_down_bytes, W_down_scale, B_down, out):
                         nc.tensor.transpose(h_ps[(g, j)][:, e, mm * P : (mm + 1) * P], words[:, e : K_PASS // 2 : 2], ident_f32[:])
 
         def copy_h(g):
-            h_grouped[g] = stage.tile([P, T * PACK], BF16, tag="h_grouped", name="h_grouped%d" % g, align_bytes=64)
+            h_grouped[g] = stage.tile([P, T * PACK], BF16, tag="h_grouped", name="h_grouped%d" % g, align_bytes=256)
             for j in range(2):
                 dst = h_grouped[g][:, j * 1024 : (j + 1) * 1024].bitcast(F32).rearrange("p (q e) -> p q e", e=2)
                 nc.scalar.copy(out=dst, in_=h_ps[(g, j)][:].rearrange("p e q -> p q e"))
 
         def quantize_h(g):
-            h_codes[g] = keep.tile([P, T], U32, name="h_codes%d" % g, align_bytes=64)
-            h_scl[g] = keep.tile([P, T], U8, name="h_scl%d" % g, align_bytes=64)
+            h_codes[g] = keep.tile([P, T], U32, name="h_codes%d" % g, align_bytes=256)
+            h_scl[g] = keep.tile([P, T], U8, name="h_scl%d" % g, align_bytes=256)
             nc.vector.quantize_mx(out=h_codes[g][:].bitcast(FP8X4), scales=h_scl[g][:], in_=h_grouped[g][:])
 
-        haT = keep.tile([P, T], BF16, name="haT")
+        haT = keep.tile([P, T], BF16, name="haT", align_bytes=256)
         haT_ps = {}
         lora_ps = {}
         lora = {}
@@ -196,7 +196,7 @@ def tile_loramlp_pb_kernel(tc, h, ha, W_down_bytes, W_down_scale, B_down, out):
             )
 
         def lora_copy(m, hf):
-            lora[(m, hf)] = keep.tile([P, N_TILE], F32, name="lora%d_%d" % (m, hf))
+            lora[(m, hf)] = keep.tile([P, N_TILE], F32, name="lora%d_%d" % (m, hf), align_bytes=256)
             nc.scalar.copy(out=lora[(m, hf)][:], in_=lora_ps[(m, hf)][:])
 
         acc = {}

from contextlib import ExitStack

import concourse.mybir as mybir
from concourse.masks import make_identity

T, D, F, R = 512, 1024, 2560, 128
FLOPS = 2 * T * F * D + 2 * T * R * D

F32 = mybir.dt.float32
BF16 = mybir.dt.bfloat16
U32 = mybir.dt.uint32
U8 = mybir.dt.uint8
FP8 = mybir.dt.float8_e4m3fn
FP8X4 = mybir.dt.float8_e4m3fn_x4
COPY = mybir.ActivationFunctionType.Copy
MULT = mybir.AluOpType.mult
ADD = mybir.AluOpType.add

P = 128
PACK = 4
K_PASS = P * PACK
PASSES = F // K_PASS
M_TILES = T // P
N_TILE = 512
HALVES = D // N_TILE
UNITS = PASSES * HALVES

V_PLANES = [2, 2, 1, 1, 1, 1, 1, 1, 2, 0]
V_COLS_LAST = 256
S_LEAD = 2
H_LAG = 1
QH_LAG = 2
HA_AT = 4
LORA0_AT = 5
LORA0_COPY_AT = 6
FINAL0_AT = 7
MX_AT = [2, 3, 4, 5, 6, 6, 6, 7, 8, 9]


def tile_loramlp_pb_kernel(tc, h, ha, W_down_bytes, W_down_scale, B_down, out):
    nc = tc.nc
    with ExitStack() as ctx:
        keep = ctx.enter_context(tc.tile_pool(name="keep", bufs=1))
        stage = ctx.enter_context(tc.tile_pool(name="stage", bufs=4))
        psum = ctx.enter_context(tc.psum_pool(name="psum", bufs=1))
        ctx.enter_context(tc.manual_schedule())

        def bank(b, shape, dtype, name):
            return psum.tile(shape, dtype, tag="bank%d" % b, name=name)

        w_view = W_down_bytes.rearrange("(g p t) n -> g p t n", p=P, t=PACK)
        s_view = W_down_scale.rearrange("(g p t) o -> g p (t o)", p=P, t=PACK)
        h_view = h.rearrange("(m p) k -> p m k", p=P)
        w_scale = {}
        w_plane = {}
        h_rows = {}

        def load_scale(g):
            w_scale[g] = keep.tile([P, PACK], F32, name="w_scale%d" % g)
            nc.sync.dma_start(out=w_scale[g][:], in_=s_view[g])

        def load_w(u, pieces):
            g, hf = u % PASSES, u // PASSES
            cols = slice(hf * N_TILE, (hf + 1) * N_TILE)
            for i in range(pieces):
                w_bytes = keep.tile([P, PACK // pieces, N_TILE], U8, name="w_bytes%d_%d" % (u, i), align_bytes=256)
                nc.sync.dma_start(out=w_bytes[:], in_=w_view[g][:, i : PACK : pieces, cols])
                for j in range(PACK // pieces):
                    w_plane[(u, i + j * pieces)] = w_bytes[:, j, :]
                if hf == 0 and i == 0:
                    load_scale(g)

        def load_h(g):
            h_rows[g] = keep.tile([P, M_TILES, K_PASS], BF16, name="h_rows%d" % g, align_bytes=256)
            nc.sync.dma_start(out=h_rows[g][:], in_=h_view[:, :, g * K_PASS : (g + 1) * K_PASS])

        ha_rows = keep.tile([P, M_TILES, R], BF16, name="ha_rows", align_bytes=256)
        b_sb = keep.tile([P, D], BF16, name="b_sb", align_bytes=256)

        load_w(0, 2)
        load_w(1, 2)
        load_w(2, 1)
        load_h(0)
        load_w(3, 1)
        load_h(1)
        load_w(4, 1)
        load_h(2)
        load_w(5, 1)
        load_h(3)
        load_w(6, 1)
        load_h(4)
        load_w(7, 1)
        nc.sync.dma_start(out=ha_rows[:], in_=ha.rearrange("(m p) r -> p m r", p=P))
        nc.sync.dma_start(out=b_sb[:], in_=B_down)
        load_w(8, 1)
        load_w(9, 1)

        ident_f32 = keep.tile([P, P], F32, name="ident_f32")
        make_identity(nc, ident_f32[:])
        ident_bf16 = keep.tile([P, P], BF16, name="ident_bf16")
        make_identity(nc, ident_bf16[:])
        warm_in = keep.tile([P, 1], F32, name="warm_in")
        warm_out = keep.tile([P, 1], F32, name="warm_out")
        nc.vector.memset(warm_in[:], 0.0)
        nc.scalar.activation(out=warm_out[:], in_=warm_in[:], func=COPY)

        wide = {}
        grouped = {}
        w_codes = {}
        w_scl = {}

        def widen_s(u):
            g = u % PASSES
            wide[u] = stage.tile([P, PACK, N_TILE], BF16, tag="wide", name="wide%d" % u, align_bytes=256)
            for t in range(PACK - V_PLANES[u]):
                nc.scalar.activation(out=wide[u][:, t, :], in_=w_plane[(u, t)].bitcast(FP8), func=COPY, scale=w_scale[g][:, t : t + 1])

        def widen_v(u):
            g = u % PASSES
            for t in range(PACK - V_PLANES[u], PACK):
                nc.vector.tensor_scalar(out=wide[u][:, t, :], in0=w_plane[(u, t)].bitcast(FP8), scalar1=w_scale[g][:, t : t + 1], scalar2=None, op0=MULT)

        def interleave_part(u, copy, lo, hi):
            copy(
                out=grouped[u][:, lo:hi, :].rearrange("p (c i) t -> p c t i", i=4),
                in_=wide[u][:, :, lo:hi].rearrange("p t (c i) -> p c t i", i=4),
            )

        def new_grouped(u):
            grouped[u] = stage.tile([P, N_TILE, PACK], BF16, tag="grouped", name="grouped%d" % u, align_bytes=256)

        def interleave(u):
            new_grouped(u)
            interleave_part(u, nc.vector.tensor_copy, 0, N_TILE)

        def quantize_w(u):
            w_codes[u] = keep.tile([P, N_TILE], U32, name="w_codes%d" % u, align_bytes=256)
            w_scl[u] = keep.tile([P, N_TILE], U8, name="w_scl%d" % u, align_bytes=256)
            nc.vector.quantize_mx(
                out=w_codes[u][:].bitcast(FP8X4),
                scales=w_scl[u][:],
                in_=grouped[u][:].rearrange("p c t -> p (c t)"),
            )

        scratch = [4]
        h_ps = {}
        h_grouped = {}
        h_codes = {}
        h_scl = {}

        def next_scratch():
            b = scratch[0]
            scratch[0] = 4 + (b - 3) % 4
            return b

        def transpose_h(g):
            for j in range(2):
                h_ps[(g, j)] = bank(next_scratch(), [P, 2, 2 * P], F32, "h_ps%d_%d" % (g, j))
                for mm in range(2):
                    words = h_rows[g][:, 2 * j + mm, :].bitcast(F32)
                    for e in range(2):
                        nc.tensor.transpose(h_ps[(g, j)][:, e, mm * P : (mm + 1) * P], words[:, e : K_PASS // 2 : 2], ident_f32[:])

        def copy_h(g):
            h_grouped[g] = stage.tile([P, T * PACK], BF16, tag="h_grouped", name="h_grouped%d" % g, align_bytes=256)
            for j in range(2):
                dst = h_grouped[g][:, j * 1024 : (j + 1) * 1024].bitcast(F32).rearrange("p (q e) -> p q e", e=2)
                nc.scalar.copy(out=dst, in_=h_ps[(g, j)][:].rearrange("p e q -> p q e"))

        def quantize_h(g):
            h_codes[g] = keep.tile([P, T], U32, name="h_codes%d" % g, align_bytes=256)
            h_scl[g] = keep.tile([P, T], U8, name="h_scl%d" % g, align_bytes=256)
            nc.vector.quantize_mx(out=h_codes[g][:].bitcast(FP8X4), scales=h_scl[g][:], in_=h_grouped[g][:])

        haT = keep.tile([P, T], BF16, name="haT", align_bytes=256)
        haT_ps = {}
        lora_ps = {}
        lora = {}

        def transpose_ha():
            haT_ps[0] = bank(next_scratch(), [P, M_TILES, P], BF16, "haT_ps")
            for m in range(M_TILES):
                nc.tensor.transpose(haT_ps[0][:, m, :], ha_rows[:, m, :], ident_bf16[:])

        def copy_haT():
            nc.scalar.copy(out=haT[:], in_=haT_ps[0][:].rearrange("p m t -> p (m t)"))

        def lora_matmul(m, hf, b):
            lora_ps[(m, hf)] = bank(b, [P, N_TILE], F32, "lora_ps%d_%d" % (m, hf))
            nc.tensor.matmul(
                lora_ps[(m, hf)][:],
                lhsT=haT[:, m * P : (m + 1) * P],
                rhs=b_sb[:, hf * N_TILE : (hf + 1) * N_TILE],
                start=True,
                stop=True,
            )

        def lora_copy(m, hf):
            lora[(m, hf)] = keep.tile([P, N_TILE], F32, name="lora%d_%d" % (m, hf), align_bytes=256)
            nc.scalar.copy(out=lora[(m, hf)][:], in_=lora_ps[(m, hf)][:])

        acc = {}

        def mx(u, tiles=(0, 1, 2, 3)):
            g, hf = u % PASSES, u // PASSES
            for m in tiles:
                if g == 0:
                    acc[(m, hf)] = bank(4 * hf + m, [P, N_TILE], F32, "acc%d_%d" % (m, hf))
                nc.tensor.matmul_mx(
                    out=acc[(m, hf)][:],
                    lhsT=h_codes[g][:, m * P : (m + 1) * P].bitcast(FP8X4),
                    lhsT_scale=h_scl[g][:, m * P : (m + 1) * P],
                    rhs=w_codes[u][:].bitcast(FP8X4),
                    rhs_scale=w_scl[u][:],
                    start=(g == 0),
                    stop=(g == PASSES - 1),
                )

        def final(m, hf):
            res = keep.tile([P, N_TILE], F32, name="res%d_%d" % (m, hf), align_bytes=256)
            nc.vector.tensor_tensor(out=res[:], in0=acc[(m, hf)][:], in1=lora[(m, hf)][:], op=ADD)
            nc.sync.dma_start(out=out[m * P : (m + 1) * P, hf * N_TILE : (hf + 1) * N_TILE], in_=res[:])

        for v in range(S_LEAD):
            widen_s(v)
        widen_v(0)
        widen_v(1)
        transpose_h(0)
        interleave(0)
        for u in range(UNITS):
            if u - H_LAG == PASSES - 1:
                copy_h(PASSES - 1)
            if u - QH_LAG == PASSES - 1:
                quantize_h(PASSES - 1)
            if u + S_LEAD < UNITS:
                widen_s(u + S_LEAD)
            if u + 2 < UNITS:
                widen_v(u + 2)
            if 0 <= u - H_LAG < PASSES - 1:
                copy_h(u - H_LAG)
                transpose_h(u - H_LAG + 1)
            if u == HA_AT:
                transpose_ha()
            if u == HA_AT + 1:
                copy_haT()
            if u == LORA0_COPY_AT:
                for m in range(M_TILES):
                    lora_copy(m, 0)
            if u == UNITS - 2:
                new_grouped(u + 1)
                interleave_part(u + 1, nc.scalar.copy, V_COLS_LAST, N_TILE)
            if u == FINAL0_AT + 1:
                lora_copy(0, 1)
                lora_copy(1, 1)
            if u < UNITS - 2:
                interleave(u + 1)
            if 0 <= u - QH_LAG < PASSES - 1:
                quantize_h(u - QH_LAG)
            quantize_w(u)
            if u == UNITS - 2:
                interleave_part(u + 1, nc.vector.tensor_copy, 0, V_COLS_LAST)
                final(2, 0)
            for v in range(UNITS - 1):
                if MX_AT[v] == u:
                    mx(v)
            if u == LORA0_AT:
                for m in range(M_TILES):
                    lora_matmul(m, 0, 4 + m)
            if u == UNITS - 2:
                lora_matmul(2, 1, 2)
            if u == UNITS - 1:
                lora_copy(2, 1)
                final(3, 0)
                mx(u, (0, 1))
                lora_matmul(3, 1, 3)
                mx(u, (2, 3))
                lora_copy(3, 1)
            if u == FINAL0_AT:
                final(0, 0)
                final(1, 0)
                lora_matmul(0, 1, 0)
                lora_matmul(1, 1, 1)
        for m in range(M_TILES):
            final(m, 1)
